import numpy as np
import ml_dtypes


def mxq(x, axis, fmt="e4m3"):
    dtype, down = {"e4m3": (ml_dtypes.float8_e4m3fn, 7), "e5m2": (ml_dtypes.float8_e5m2, 14)}[fmt]
    v = np.moveaxis(np.asarray(x, np.float32).astype(ml_dtypes.bfloat16).astype(np.float64), axis, -1)
    blocks = v.reshape(v.shape[:-1] + (-1, 32))
    amax = np.abs(blocks).max(-1, keepdims=True)
    byte = np.maximum(np.where(amax > 0, np.frexp(amax)[1] - 1 + 127, 0) - down, 1)
    scale = np.exp2(byte - 127.0)
    codes = (blocks / scale).astype(np.float32).astype(dtype).astype(np.float64)
    return np.moveaxis((codes * scale).reshape(v.shape), -1, axis)


WIDE = False


def mx_kscale(k):
    if not WIDE:
        return np.ones(k)
    levels = np.array([10, -10, 5, -5, 0])
    a = np.random.permutation(np.resize(levels, k // 512 * 4)).reshape(k // 512, 4)
    idx = np.arange(k)
    return np.exp2(a[idx // 512, idx % 128 // 32])


BF16 = ml_dtypes.bfloat16


def bf(x):
    return np.asarray(x, np.float32).astype(BF16)


def f64(x):
    return np.asarray(x).astype(np.float64)


B, D_IN, D_H = 512, 1024, 1024


def sigmoid(v):
    return 1.0 / (1.0 + np.exp(-v))


def setup_inputs():
    s, t = mx_kscale(D_IN), mx_kscale(D_H)
    fg = np.exp(0.75 * np.random.standard_normal((B, D_H)))
    ig = np.exp(0.75 * np.random.standard_normal((B, D_H)))
    c = fg * np.random.standard_normal((B, D_H)) + ig * np.tanh(0.75 * np.random.standard_normal((B, D_H)))
    n = fg * np.random.uniform(size=(B, D_H)) + ig
    return {"x": bf(np.random.standard_normal((B, D_IN)) * s),
            "h_prev": bf(np.random.standard_normal((B, D_H)) * t),
            "c": bf(c),
            "n": bf(n),
            "W_o": bf(np.random.standard_normal((D_IN, D_H)) * 0.5 / np.sqrt(D_IN) / s[:, None]),
            "b_o": bf(np.random.standard_normal(D_H) * 0.3),
            "U_o": bf(np.random.standard_normal((D_H, D_H)) * 0.5 / np.sqrt(D_H) / t[:, None])}


def reference(x, h_prev, c, n, W_o, b_o, U_o):
    o = sigmoid((mxq(f64(x), 1, "e4m3") @ mxq(f64(W_o), 0, "e4m3")) + f64(b_o) + (mxq(f64(h_prev), 1, "e4m3") @ mxq(f64(U_o), 0, "e4m3")))
    return o * (f64(c) / (f64(n) + 1e-6))

@@ -1,0 +1,186 @@
+from contextlib import ExitStack
+
+import concourse.masks as masks
+import concourse.mybir as mybir
+
+F32 = mybir.dt.float32
+BF16 = mybir.dt.bfloat16
+U32 = mybir.dt.uint32
+U8 = mybir.dt.uint8
+FP8X4 = mybir.dt.float8_e4m3fn_x4
+ACT = mybir.ActivationFunctionType
+ALU = mybir.AluOpType
+
+P = 128
+BATCH = 512
+FEAT = 1024
+NB = BATCH // P
+NJ = FEAT // P
+PASSES = 4
+S_COLS = 192
+
+FLOPS = 2 * BATCH * FEAT * FEAT * 2
+
+
+def tile_slstmcell_pb_kernel(tc, x, h_prev, c, n, W_o, b_o, U_o, out):
+    nc = tc.nc
+    with ExitStack() as ctx:
+        keep = ctx.enter_context(tc.tile_pool(name="keep", bufs=1))
+        psum = ctx.enter_context(tc.psum_pool(name="psum", bufs=1))
+
+        ident = keep.tile([P, P], F32, name="ident")
+        masks.make_identity(nc, ident[:])
+        eps_t = keep.tile([P, 1], F32, name="eps_t")
+        nc.vector.memset(eps_t[:], 1e-6)
+        b_rows = keep.tile([P, P], BF16, name="b_rows")
+        nc.vector.memset(b_rows[:], 0.0)
+
+        n_sb = keep.tile([P, NB, FEAT], BF16, name="n_sb")
+        c_sb = keep.tile([P, NB, FEAT], BF16, name="c_sb")
+        a_sb = [keep.tile([P, NB, FEAT], BF16, name="a_sb%d" % o) for o in range(2)]
+        raw = [keep.tile([P, 4, FEAT], BF16, name="raw%d" % g) for g in range(PASSES)]
+        wg = [keep.tile([P, FEAT, 4], BF16, name="wg%d" % g, align_bytes=64) for g in range(PASSES)]
+        wc = keep.tile([P, PASSES, FEAT], U32, name="wc", align_bytes=64)
+        ws = keep.tile([P, PASSES, FEAT], U8, name="ws", align_bytes=64)
+        xg = [keep.tile([P, BATCH * 4], BF16, name="xg%d" % g, align_bytes=64) for g in range(PASSES)]
+        xc = keep.tile([P, PASSES, BATCH], U32, name="xc", align_bytes=64)
+        xs = keep.tile([P, PASSES, BATCH], U8, name="xs", align_bytes=64)
+        rq = keep.tile([P, NB, FEAT], F32, name="rq")
+        ot = [keep.tile([P, BATCH], F32, name="ot%d" % j) for j in range(NJ)]
+        ho = keep.tile([P, NB, FEAT], F32, name="ho")
+
+        acts = [x, h_prev]
+        wts = [W_o, U_o]
+        n_v = n.rearrange("(p b) d -> p b d", b=NB)
+        c_v = c.rearrange("(p b) d -> p b d", b=NB)
+        out_v = out.rearrange("(p b) d -> p b d", b=NB)
+
+        def load_w(g):
+            src = wts[g // 2][512 * (g % 2) : 512 * (g % 2) + 512, :]
+            nc.sync.dma_start(
+                out=raw[g][:].rearrange("p (u e) w -> p u e w", u=2),
+                in_=src.rearrange("(u q e) w -> q u e w", u=2, e=2),
+            )
+
+        def load_a(o, bp):
+            nc.sync.dma_start(
+                out=a_sb[o][:, 2 * bp : 2 * bp + 2, :],
+                in_=acts[o].rearrange("(p b) k -> p b k", b=NB)[:, 2 * bp : 2 * bp + 2, :],
+            )
+
+        nc.sync.dma_start(out=n_sb[:, 0:1, :], in_=n_v[:, 0:1, :])
+        load_w(0)
+        nc.sync.dma_start(out=b_rows[0:NJ, :], in_=b_o.rearrange("(j p) -> j p", p=P))
+        for b in range(1, NB):
+            nc.sync.dma_start(out=n_sb[:, b : b + 1, :], in_=n_v[:, b : b + 1, :])
+        load_w(1)
+        load_a(0, 0)
+        load_a(0, 1)
+        load_w(2)
+        load_a(1, 0)
+        load_a(1, 1)
+        load_w(3)
+        for b in range(NB):
+            nc.sync.dma_start(out=c_sb[:, b : b + 1, :], in_=c_v[:, b : b + 1, :])
+
+        def ln(b):
+            nc.scalar.activation(out=rq[:, b, :], in_=n_sb[:, b, :], func=ACT.Ln, bias=eps_t[:, 0:1], scale=1.0)
+
+        def regroup(g):
+            v = FEAT - S_COLS
+            nc.vector.tensor_copy(
+                out=wg[g][:, 0:v, :].rearrange("p (c i) t -> p c t i", i=4),
+                in_=raw[g][:, :, 0:v].rearrange("p t (c i) -> p c t i", i=4),
+            )
+            nc.scalar.copy(
+                out=wg[g][:, v:FEAT, :].rearrange("p (c i) t -> p c t i", i=4),
+                in_=raw[g][:, :, v:FEAT].rearrange("p t (c i) -> p c t i", i=4),
+            )
+
+        def quant_w(g):
+            nc.vector.quantize_mx(
+                out=wc[:, g, :].bitcast(FP8X4),
+                scales=ws[:, g, :],
+                in_=wg[g][:].rearrange("p w t -> p (w t)"),
+            )
+
+        def flip(g):
+            o, gp = g // 2, g % 2
+            for bp in range(2):
+                xt = psum.tile([P, 2, 2 * P], F32, name="xt%d_%d" % (g, bp), tag="bank%d" % (2 * g + bp))
+                for u in range(2):
+                    for bl in range(2):
+                        words = a_sb[o][:, 2 * bp + bl, :].bitcast(F32)
+                        nc.tensor.transpose(
+                            xt[:, u, bl * P : (bl + 1) * P],
+                            words[:, 256 * gp + P * u : 256 * gp + P * u + P],
+                            ident[:],
+                        )
+                dst = xg[g][:].bitcast(F32).rearrange("p (r u) -> p r u", u=2)
+                nc.scalar.copy(
+                    out=dst[:, 2 * P * bp : 2 * P * (bp + 1), :],
+                    in_=xt[:].rearrange("p u r -> p r u"),
+                )
+
+        def quant_x(g):
+            nc.vector.quantize_mx(out=xc[:, g, :].bitcast(FP8X4), scales=xs[:, g, :], in_=xg[g][:])
+
+        b_f32 = keep.tile([P, P], F32, name="b_f32")
+        nc.vector.tensor_copy(out=b_f32[:], in_=b_rows[:])
+        b_ps = psum.tile([P, P], F32, name="b_ps", tag="bank7")
+        nc.tensor.transpose(b_ps[:], b_f32[:], ident[:])
+        b_half = keep.tile([P, NJ], F32, name="b_half")
+        nc.vector.tensor_scalar_mul(out=b_half[:], in0=b_ps[:, 0:NJ], scalar1=0.5)
+
+        ln(0)
+        regroup(0)
+        for b in range(1, NB):
+            ln(b)
+        regroup(1)
+        quant_w(0)
+        flip(0)
+        flip(1)
+        quant_w(1)
+        regroup(2)
+        quant_x(0)
+        quant_x(1)
+        flip(2)
+        flip(3)
+        quant_w(2)
+        regroup(3)
+        quant_x(2)
+        quant_x(3)
+        quant_w(3)
+
+        acc = [psum.tile([P, BATCH], F32, name="acc%d" % j, tag="bank%d" % j) for j in range(NJ)]
+        for g in range(PASSES):
+            for j in range(NJ):
+                nc.tensor.matmul_mx(
+                    out=acc[j][:],
+                    lhsT=wc[:, g, j * P : (j + 1) * P].bitcast(FP8X4),
+                    lhsT_scale=ws[:, g, j * P : (j + 1) * P],
+                    rhs=xc[:, g, :].bitcast(FP8X4),
+                    rhs_scale=xs[:, g, :],
+                    start=(g == 0),
+                    stop=(g == PASSES - 1),
+                )
+
+        for k in range(4):
+            cols = slice(256 * k, 256 * (k + 1))
+            nc.scalar.activation(out=rq[:, :, cols], in_=rq[:, :, cols], func=ACT.Exp, scale=-1.0)
+            nc.vector.scalar_tensor_tensor(
+                out=rq[:, :, cols], in0=c_sb[:, :, cols], scalar=0.5, in1=rq[:, :, cols], op0=ALU.mult, op1=ALU.mult
+            )
+
+        for j in range(NJ):
+            nc.scalar.activation(out=ot[j][:], in_=acc[j][:], func=ACT.Tanh, bias=b_half[:, j : j + 1], scale=0.5)
+            tp = psum.tile([P, NB, P], F32, name="tp%d" % j, tag="bank%d" % j)
+            for b in range(NB):
+                nc.tensor.transpose(tp[:, b, :], ot[j][:, b * P : (b + 1) * P], ident[:])
+            cols = slice(j * P, (j + 1) * P)
+            nc.vector.scalar_tensor_tensor(
+                out=ho[:, :, cols], in0=tp[:], scalar=1.0, in1=rq[:, :, cols], op0=ALU.add, op1=ALU.mult
+            )
+            if j % 2 == 1:
+                pair = slice((j - 1) * P, (j + 1) * P)
+                nc.sync.dma_start(out=out_v[:, :, pair], in_=ho[:, :, pair])

@@ -17,7 +17,6 @@ FEAT = 1024
 NB = BATCH // P
 NJ = FEAT // P
 PASSES = 4
-S_COLS = 192
 
 FLOPS = 2 * BATCH * FEAT * FEAT * 2
 
@@ -30,8 +29,8 @@ def tile_slstmcell_pb_kernel(tc, x, h_prev, c, n, W_o, b_o, U_o, out):
 
         ident = keep.tile([P, P], F32, name="ident")
         masks.make_identity(nc, ident[:])
-        eps_t = keep.tile([P, 1], F32, name="eps_t")
-        nc.vector.memset(eps_t[:], 1e-6)
+        eps2 = keep.tile([P, 1], F32, name="eps2")
+        nc.vector.memset(eps2[:], 2e-6)
         b_rows = keep.tile([P, P], BF16, name="b_rows")
         nc.vector.memset(b_rows[:], 0.0)
 
@@ -48,139 +47,246 @@ def tile_slstmcell_pb_kernel(tc, x, h_prev, c, n, W_o, b_o, U_o, out):
         rq = keep.tile([P, NB, FEAT], F32, name="rq")
         ot = [keep.tile([P, BATCH], F32, name="ot%d" % j) for j in range(NJ)]
         ho = keep.tile([P, NB, FEAT], F32, name="ho")
-
-        acts = [x, h_prev]
+        b_f32 = keep.tile([P, P], F32, name="b_f32")
+        b_half = keep.tile([P, NJ], F32, name="b_half")
+        b_ps = psum.tile([P, P], F32, name="b_ps", tag="bank7")
         wts = [W_o, U_o]
-        n_v = n.rearrange("(p b) d -> p b d", b=NB)
-        c_v = c.rearrange("(p b) d -> p b d", b=NB)
         out_v = out.rearrange("(p b) d -> p b d", b=NB)
+        xt = {}
+        acc = {}
+        tp = {}
 
-        def load_w(g):
+        def load_w(g, lo, hi):
             src = wts[g // 2][512 * (g % 2) : 512 * (g % 2) + 512, :]
-            nc.sync.dma_start(
-                out=raw[g][:].rearrange("p (u e) w -> p u e w", u=2),
-                in_=src.rearrange("(u q e) w -> q u e w", u=2, e=2),
-            )
+            if hi - lo == FEAT:
+                nc.sync.dma_start(
+                    out=raw[g][:].rearrange("p (u e) w -> p u e w", u=2),
+                    in_=src.rearrange("(u q e) w -> q u e w", u=2, e=2),
+                )
+            else:
+                for u in range(2):
+                    nc.sync.dma_start(
+                        out=raw[g][:, 2 * u : 2 * u + 2, lo:hi],
+                        in_=src[256 * u : 256 * u + 256, lo:hi].rearrange("(q e) w -> q e w", e=2),
+                    )
 
-        def load_a(o, bp):
-            nc.sync.dma_start(
-                out=a_sb[o][:, 2 * bp : 2 * bp + 2, :],
-                in_=acts[o].rearrange("(p b) k -> p b k", b=NB)[:, 2 * bp : 2 * bp + 2, :],
-            )
+        def load_rows(dst, src, lo, hi):
+            nc.sync.dma_start(out=dst[:, lo:hi, :], in_=src.rearrange("(p b) d -> p b d", b=NB)[:, lo:hi, :])
 
-        nc.sync.dma_start(out=n_sb[:, 0:1, :], in_=n_v[:, 0:1, :])
-        load_w(0)
-        nc.sync.dma_start(out=b_rows[0:NJ, :], in_=b_o.rearrange("(j p) -> j p", p=P))
-        for b in range(1, NB):
-            nc.sync.dma_start(out=n_sb[:, b : b + 1, :], in_=n_v[:, b : b + 1, :])
-        load_w(1)
-        load_a(0, 0)
-        load_a(0, 1)
-        load_w(2)
-        load_a(1, 0)
-        load_a(1, 1)
-        load_w(3)
-        for b in range(NB):
-            nc.sync.dma_start(out=c_sb[:, b : b + 1, :], in_=c_v[:, b : b + 1, :])
+        def load_bias():
+            nc.sync.dma_start(out=b_rows[0:NJ, :], in_=b_o.rearrange("(j p) -> j p", p=P))
+
+        def bias_cast():
+            nc.vector.tensor_copy(out=b_f32[:], in_=b_rows[:])
+
+        def bias_flip():
+            nc.tensor.transpose(b_ps[:], b_f32[:], ident[:])
+
+        def bias_halve():
+            nc.vector.tensor_scalar_mul(out=b_half[:], in0=b_ps[:, 0:NJ], scalar1=0.5)
 
         def ln(b):
-            nc.scalar.activation(out=rq[:, b, :], in_=n_sb[:, b, :], func=ACT.Ln, bias=eps_t[:, 0:1], scale=1.0)
+            nc.scalar.activation(out=rq[:, b, :], in_=n_sb[:, b, :], func=ACT.Ln, bias=eps2[:, 0:1], scale=2.0)
 
-        def regroup(g):
-            v = FEAT - S_COLS
-            nc.vector.tensor_copy(
-                out=wg[g][:, 0:v, :].rearrange("p (c i) t -> p c t i", i=4),
-                in_=raw[g][:, :, 0:v].rearrange("p t (c i) -> p c t i", i=4),
-            )
-            nc.scalar.copy(
-                out=wg[g][:, v:FEAT, :].rearrange("p (c i) t -> p c t i", i=4),
-                in_=raw[g][:, :, v:FEAT].rearrange("p t (c i) -> p c t i", i=4),
+        def ex(b):
+            nc.scalar.activation(out=rq[:, b, :], in_=rq[:, b, :], func=ACT.Exp, scale=-1.0)
+
+        def cr(b):
+            nc.vector.tensor_tensor(out=rq[:, b, :], in0=c_sb[:, b, :], in1=rq[:, b, :], op=ALU.mult)
+
+        def regroup(copy, g, lo, hi):
+            copy(
+                out=wg[g][:, lo:hi, :].rearrange("p (c i) t -> p c t i", i=4),
+                in_=raw[g][:, :, lo:hi].rearrange("p t (c i) -> p c t i", i=4),
             )
 
-        def quant_w(g):
+        def quant_w(g, lo, hi):
             nc.vector.quantize_mx(
-                out=wc[:, g, :].bitcast(FP8X4),
-                scales=ws[:, g, :],
-                in_=wg[g][:].rearrange("p w t -> p (w t)"),
+                out=wc[:, g, lo:hi].bitcast(FP8X4),
+                scales=ws[:, g, lo:hi],
+                in_=wg[g][:, lo:hi, :].rearrange("p w t -> p (w t)"),
             )
 
-        def flip(g):
+        def flip(g, bp):
             o, gp = g // 2, g % 2
-            for bp in range(2):
-                xt = psum.tile([P, 2, 2 * P], F32, name="xt%d_%d" % (g, bp), tag="bank%d" % (2 * g + bp))
-                for u in range(2):
-                    for bl in range(2):
-                        words = a_sb[o][:, 2 * bp + bl, :].bitcast(F32)
-                        nc.tensor.transpose(
-                            xt[:, u, bl * P : (bl + 1) * P],
-                            words[:, 256 * gp + P * u : 256 * gp + P * u + P],
-                            ident[:],
-                        )
-                dst = xg[g][:].bitcast(F32).rearrange("p (r u) -> p r u", u=2)
-                nc.scalar.copy(
-                    out=dst[:, 2 * P * bp : 2 * P * (bp + 1), :],
-                    in_=xt[:].rearrange("p u r -> p r u"),
-                )
+            t = psum.tile([P, 2, 2 * P], F32, name="xt%d_%d" % (g, bp), tag="bank%d" % (2 * g + bp))
+            xt[(g, bp)] = t
+            for u in range(2):
+                for bl in range(2):
+                    words = a_sb[o][:, 2 * bp + bl, :].bitcast(F32)
+                    nc.tensor.transpose(
+                        t[:, u, bl * P : (bl + 1) * P],
+                        words[:, 256 * gp + P * u : 256 * gp + P * u + P],
+                        ident[:],
+                    )
+
+        def flip_out(copy, g, bp):
+            dst = xg[g][:].bitcast(F32).rearrange("p (r u) -> p r u", u=2)
+            copy(out=dst[:, 2 * P * bp : 2 * P * (bp + 1), :], in_=xt[(g, bp)][:].rearrange("p u r -> p r u"))
 
         def quant_x(g):
             nc.vector.quantize_mx(out=xc[:, g, :].bitcast(FP8X4), scales=xs[:, g, :], in_=xg[g][:])
 
-        b_f32 = keep.tile([P, P], F32, name="b_f32")
-        nc.vector.tensor_copy(out=b_f32[:], in_=b_rows[:])
-        b_ps = psum.tile([P, P], F32, name="b_ps", tag="bank7")
-        nc.tensor.transpose(b_ps[:], b_f32[:], ident[:])
-        b_half = keep.tile([P, NJ], F32, name="b_half")
-        nc.vector.tensor_scalar_mul(out=b_half[:], in0=b_ps[:, 0:NJ], scalar1=0.5)
-
-        ln(0)
-        regroup(0)
-        for b in range(1, NB):
-            ln(b)
-        regroup(1)
-        quant_w(0)
-        flip(0)
-        flip(1)
-        quant_w(1)
-        regroup(2)
-        quant_x(0)
-        quant_x(1)
-        flip(2)
-        flip(3)
-        quant_w(2)
-        regroup(3)
-        quant_x(2)
-        quant_x(3)
-        quant_w(3)
-
-        acc = [psum.tile([P, BATCH], F32, name="acc%d" % j, tag="bank%d" % j) for j in range(NJ)]
-        for g in range(PASSES):
-            for j in range(NJ):
-                nc.tensor.matmul_mx(
-                    out=acc[j][:],
-                    lhsT=wc[:, g, j * P : (j + 1) * P].bitcast(FP8X4),
-                    lhsT_scale=ws[:, g, j * P : (j + 1) * P],
-                    rhs=xc[:, g, :].bitcast(FP8X4),
-                    rhs_scale=xs[:, g, :],
-                    start=(g == 0),
-                    stop=(g == PASSES - 1),
-                )
-
-        for k in range(4):
-            cols = slice(256 * k, 256 * (k + 1))
-            nc.scalar.activation(out=rq[:, :, cols], in_=rq[:, :, cols], func=ACT.Exp, scale=-1.0)
-            nc.vector.scalar_tensor_tensor(
-                out=rq[:, :, cols], in0=c_sb[:, :, cols], scalar=0.5, in1=rq[:, :, cols], op0=ALU.mult, op1=ALU.mult
+        def mx(g, j):
+            if g == 0:
+                acc[j] = psum.tile([P, BATCH], F32, name="acc%d" % j, tag="bank%d" % j)
+            nc.tensor.matmul_mx(
+                out=acc[j][:],
+                lhsT=wc[:, g, j * P : (j + 1) * P].bitcast(FP8X4),
+                lhsT_scale=ws[:, g, j * P : (j + 1) * P],
+                rhs=xc[:, g, :].bitcast(FP8X4),
+                rhs_scale=xs[:, g, :],
+                start=(g == 0),
+                stop=(g == PASSES - 1),
             )
 
-        for j in range(NJ):
+        def th(j):
             nc.scalar.activation(out=ot[j][:], in_=acc[j][:], func=ACT.Tanh, bias=b_half[:, j : j + 1], scale=0.5)
-            tp = psum.tile([P, NB, P], F32, name="tp%d" % j, tag="bank%d" % j)
+
+        def to(j):
+            tp[j] = psum.tile([P, NB, P], F32, name="tp%d" % j, tag="bank%d" % j)
             for b in range(NB):
-                nc.tensor.transpose(tp[:, b, :], ot[j][:, b * P : (b + 1) * P], ident[:])
+                nc.tensor.transpose(tp[j][:, b, :], ot[j][:, b * P : (b + 1) * P], ident[:])
+
+        def fm(j):
             cols = slice(j * P, (j + 1) * P)
             nc.vector.scalar_tensor_tensor(
-                out=ho[:, :, cols], in0=tp[:], scalar=1.0, in1=rq[:, :, cols], op0=ALU.add, op1=ALU.mult
+                out=ho[:, :, cols], in0=tp[j][:], scalar=1.0, in1=rq[:, :, cols], op0=ALU.add, op1=ALU.mult
             )
-            if j % 2 == 1:
-                pair = slice((j - 1) * P, (j + 1) * P)
-                nc.sync.dma_start(out=out_v[:, :, pair], in_=ho[:, :, pair])
+
+        def store(j0, j1):
+            cols = slice(j0 * P, j1 * P)
+            nc.sync.dma_start(out=out_v[:, :, cols], in_=ho[:, :, cols])
+
+        with tc.manual_schedule():
+            load_w(0, 0, 512)
+            load_rows(n_sb, n, 0, 1)
+            load_bias()
+            load_w(0, 512, 1024)
+            load_rows(n_sb, n, 1, 2)
+            load_rows(n_sb, n, 2, 3)
+            load_rows(n_sb, n, 3, 4)
+            load_w(1, 0, FEAT)
+            load_rows(a_sb[0], x, 0, 2)
+            load_rows(a_sb[0], x, 2, 4)
+            load_w(2, 0, FEAT)
+            load_rows(a_sb[1], h_prev, 0, 2)
+            load_rows(a_sb[1], h_prev, 2, 4)
+            load_w(3, 0, 512)
+            load_w(3, 512, 1024)
+            load_rows(c_sb, c, 0, 1)
+            load_rows(c_sb, c, 1, 2)
+            load_rows(c_sb, c, 2, 3)
+            load_rows(c_sb, c, 3, 4)
+            regroup(nc.vector.tensor_copy, 0, 0, 512)
+            ln(0)
+            bias_cast()
+            quant_w(0, 0, 512)
+            bias_flip()
+            regroup(nc.vector.tensor_copy, 0, 512, 1024)
+            ln(1)
+            bias_halve()
+            quant_w(0, 512, 1024)
+            ln(2)
+            ln(3)
+            regroup(nc.vector.tensor_copy, 1, 0, 928)
+            regroup(nc.scalar.copy, 1, 928, 1024)
+            flip(0, 0)
+            flip(1, 0)
+            flip(0, 1)
+            quant_w(1, 0, 1024)
+            flip_out(nc.scalar.copy, 0, 0)
+            flip(1, 1)
+            flip_out(nc.scalar.copy, 0, 1)
+            flip_out(nc.scalar.copy, 1, 0)
+            quant_x(0)
+            flip_out(nc.scalar.copy, 1, 1)
+            regroup(nc.vector.tensor_copy, 2, 0, 768)
+            mx(0, 0)
+            regroup(nc.scalar.copy, 2, 768, 1024)
+            mx(0, 1)
+            mx(0, 2)
+            flip(2, 0)
+            ex(0)
+            quant_x(1)
+            flip(3, 0)
+            mx(0, 3)
+            quant_w(2, 0, 1024)
+            flip(2, 1)
+            flip_out(nc.scalar.copy, 2, 0)
+            flip(3, 1)
+            mx(1, 0)
+            flip_out(nc.scalar.copy, 2, 1)
+            regroup(nc.vector.tensor_copy, 3, 0, 336)
+            mx(1, 1)
+            flip_out(nc.scalar.copy, 3, 0)
+            mx(1, 2)
+            mx(0, 4)
+            quant_x(2)
+            mx(1, 3)
+            flip_out(nc.scalar.copy, 3, 1)
+            mx(0, 5)
+            regroup(nc.vector.tensor_copy, 3, 512, 848)
+            mx(1, 4)
+            regroup(nc.scalar.copy, 3, 336, 512)
+            mx(0, 6)
+            mx(1, 5)
+            quant_x(3)
+            mx(0, 7)
+            regroup(nc.scalar.copy, 3, 848, 1024)
+            mx(1, 6)
+            quant_w(3, 0, 512)
+            mx(2, 0)
+            mx(1, 7)
+            ex(1)
+            cr(0)
+            mx(2, 1)
+            mx(2, 2)
+            mx(2, 3)
+            mx(2, 4)
+            ex(2)
+            quant_w(3, 512, 1024)
+            mx(2, 5)
+            mx(2, 6)
+            cr(1)
+            mx(2, 7)
+            mx(3, 0)
+            ex(3)
+            mx(3, 1)
+            mx(3, 2)
+            cr(2)
+            mx(3, 3)
+            mx(3, 4)
+            th(0)
+            mx(3, 5)
+            mx(3, 6)
+            th(1)
+            cr(3)
+            mx(3, 7)
+            to(0)
+            th(2)
+            to(1)
+            th(3)
+            to(2)
+            fm(0)
+            th(4)
+            to(3)
+            fm(1)
+            th(5)
+            to(4)
+            fm(2)
+            store(0, 2)
+            th(6)
+            to(5)
+            fm(3)
+            th(7)
+            to(6)
+            fm(4)
+            store(2, 4)
+            to(7)
+            fm(5)
+            fm(6)
+            store(4, 6)
+            fm(7)
+            store(6, 7)
+            store(7, 8)

@@ -16,7 +16,11 @@ BATCH = 512
 FEAT = 1024
 NB = BATCH // P
 NJ = FEAT // P
-PASSES = 4
+K_PASS = 4 * P
+PASSES = 2 * FEAT // K_PASS
+EPS = 1e-6
+
+SCALAR_COLS = (0, 0, 256, 512)
 
 FLOPS = 2 * BATCH * FEAT * FEAT * 2
 
@@ -30,263 +34,175 @@ def tile_slstmcell_pb_kernel(tc, x, h_prev, c, n, W_o, b_o, U_o, out):
         ident = keep.tile([P, P], F32, name="ident")
         masks.make_identity(nc, ident[:])
         eps2 = keep.tile([P, 1], F32, name="eps2")
-        nc.vector.memset(eps2[:], 2e-6)
-        b_rows = keep.tile([P, P], BF16, name="b_rows")
-        nc.vector.memset(b_rows[:], 0.0)
+        nc.vector.memset(eps2[:], 2.0 * EPS)
+        bias_rows = keep.tile([P, P], BF16, name="bias_rows")
+        nc.vector.memset(bias_rows[:], 0.0)
 
+        acts = [x, h_prev]
+        weights = [W_o, U_o]
+        act_sb = [keep.tile([P, NB, FEAT], BF16, name="act_sb%d" % o) for o in range(2)]
         n_sb = keep.tile([P, NB, FEAT], BF16, name="n_sb")
         c_sb = keep.tile([P, NB, FEAT], BF16, name="c_sb")
-        a_sb = [keep.tile([P, NB, FEAT], BF16, name="a_sb%d" % o) for o in range(2)]
-        raw = [keep.tile([P, 4, FEAT], BF16, name="raw%d" % g) for g in range(PASSES)]
-        wg = [keep.tile([P, FEAT, 4], BF16, name="wg%d" % g, align_bytes=64) for g in range(PASSES)]
-        wc = keep.tile([P, PASSES, FEAT], U32, name="wc", align_bytes=64)
-        ws = keep.tile([P, PASSES, FEAT], U8, name="ws", align_bytes=64)
-        xg = [keep.tile([P, BATCH * 4], BF16, name="xg%d" % g, align_bytes=64) for g in range(PASSES)]
-        xc = keep.tile([P, PASSES, BATCH], U32, name="xc", align_bytes=64)
-        xs = keep.tile([P, PASSES, BATCH], U8, name="xs", align_bytes=64)
-        rq = keep.tile([P, NB, FEAT], F32, name="rq")
-        ot = [keep.tile([P, BATCH], F32, name="ot%d" % j) for j in range(NJ)]
-        ho = keep.tile([P, NB, FEAT], F32, name="ho")
-        b_f32 = keep.tile([P, P], F32, name="b_f32")
-        b_half = keep.tile([P, NJ], F32, name="b_half")
-        b_ps = psum.tile([P, P], F32, name="b_ps", tag="bank7")
-        wts = [W_o, U_o]
-        out_v = out.rearrange("(p b) d -> p b d", b=NB)
-        xt = {}
+        w_rows = [keep.tile([P, 4, FEAT], BF16, name="w_rows%d" % g) for g in range(PASSES)]
+        w_words = [keep.tile([P, FEAT, 4], BF16, name="w_words%d" % g, align_bytes=64) for g in range(PASSES)]
+        w_codes = keep.tile([P, PASSES, FEAT], U32, name="w_codes", align_bytes=64)
+        w_scales = keep.tile([P, PASSES, FEAT], U8, name="w_scales", align_bytes=64)
+        a_words = [keep.tile([P, BATCH * 4], BF16, name="a_words%d" % g, align_bytes=64) for g in range(PASSES)]
+        a_codes = keep.tile([P, PASSES, BATCH], U32, name="a_codes", align_bytes=64)
+        a_scales = keep.tile([P, PASSES, BATCH], U8, name="a_scales", align_bytes=64)
+        ratio = keep.tile([P, NB, FEAT], F32, name="ratio")
+        gate_t = [keep.tile([P, BATCH], F32, name="gate_t%d" % j) for j in range(NJ)]
+        h_sb = keep.tile([P, NB, FEAT], F32, name="h_sb")
+        bias_f32 = keep.tile([P, P], F32, name="bias_f32")
+        bias_half = keep.tile([P, NJ], F32, name="bias_half")
+        bias_ps = psum.tile([P, P], F32, name="bias_ps", tag="bank7")
+        flipped = {}
         acc = {}
-        tp = {}
+        gate = {}
 
-        def load_w(g, lo, hi):
-            src = wts[g // 2][512 * (g % 2) : 512 * (g % 2) + 512, :]
-            if hi - lo == FEAT:
-                nc.sync.dma_start(
-                    out=raw[g][:].rearrange("p (u e) w -> p u e w", u=2),
-                    in_=src.rearrange("(u q e) w -> q u e w", u=2, e=2),
-                )
-            else:
-                for u in range(2):
-                    nc.sync.dma_start(
-                        out=raw[g][:, 2 * u : 2 * u + 2, lo:hi],
-                        in_=src[256 * u : 256 * u + 256, lo:hi].rearrange("(q e) w -> q e w", e=2),
-                    )
+        def by_partition(rows):
+            return rows.rearrange("(p b) d -> p b d", b=NB)
 
         def load_rows(dst, src, lo, hi):
-            nc.sync.dma_start(out=dst[:, lo:hi, :], in_=src.rearrange("(p b) d -> p b d", b=NB)[:, lo:hi, :])
+            nc.sync.dma_start(out=dst[:, lo:hi, :], in_=by_partition(src)[:, lo:hi, :])
 
-        def load_bias():
-            nc.sync.dma_start(out=b_rows[0:NJ, :], in_=b_o.rearrange("(j p) -> j p", p=P))
-
-        def bias_cast():
-            nc.vector.tensor_copy(out=b_f32[:], in_=b_rows[:])
-
-        def bias_flip():
-            nc.tensor.transpose(b_ps[:], b_f32[:], ident[:])
-
-        def bias_halve():
-            nc.vector.tensor_scalar_mul(out=b_half[:], in0=b_ps[:, 0:NJ], scalar1=0.5)
-
-        def ln(b):
-            nc.scalar.activation(out=rq[:, b, :], in_=n_sb[:, b, :], func=ACT.Ln, bias=eps2[:, 0:1], scale=2.0)
-
-        def ex(b):
-            nc.scalar.activation(out=rq[:, b, :], in_=rq[:, b, :], func=ACT.Exp, scale=-1.0)
-
-        def cr(b):
-            nc.vector.tensor_tensor(out=rq[:, b, :], in0=c_sb[:, b, :], in1=rq[:, b, :], op=ALU.mult)
-
-        def regroup(copy, g, lo, hi):
-            copy(
-                out=wg[g][:, lo:hi, :].rearrange("p (c i) t -> p c t i", i=4),
-                in_=raw[g][:, :, lo:hi].rearrange("p t (c i) -> p c t i", i=4),
-            )
-
-        def quant_w(g, lo, hi):
-            nc.vector.quantize_mx(
-                out=wc[:, g, lo:hi].bitcast(FP8X4),
-                scales=ws[:, g, lo:hi],
-                in_=wg[g][:, lo:hi, :].rearrange("p w t -> p (w t)"),
-            )
-
-        def flip(g, bp):
-            o, gp = g // 2, g % 2
-            t = psum.tile([P, 2, 2 * P], F32, name="xt%d_%d" % (g, bp), tag="bank%d" % (2 * g + bp))
-            xt[(g, bp)] = t
+        def load_weights(g, lo, hi):
+            rows = weights[g // 2][K_PASS * (g % 2) : K_PASS * (g % 2 + 1), :]
             for u in range(2):
-                for bl in range(2):
-                    words = a_sb[o][:, 2 * bp + bl, :].bitcast(F32)
-                    nc.tensor.transpose(
-                        t[:, u, bl * P : (bl + 1) * P],
-                        words[:, 256 * gp + P * u : 256 * gp + P * u + P],
-                        ident[:],
+                nc.sync.dma_start(
+                    out=w_rows[g][:, 2 * u : 2 * u + 2, lo:hi],
+                    in_=rows[2 * P * u : 2 * P * (u + 1), lo:hi].rearrange("(p e) w -> p e w", e=2),
+                )
+
+        def interleave(g, lo, hi):
+            cut = hi - SCALAR_COLS[g] * (hi - lo) // FEAT
+            for copy, a, b in ((nc.vector.tensor_copy, lo, cut), (nc.scalar.copy, cut, hi)):
+                if b > a:
+                    copy(
+                        out=w_words[g][:, a:b, :].rearrange("p (w i) t -> p w t i", i=4),
+                        in_=w_rows[g][:, :, a:b].rearrange("p t (w i) -> p w t i", i=4),
                     )
 
-        def flip_out(copy, g, bp):
-            dst = xg[g][:].bitcast(F32).rearrange("p (r u) -> p r u", u=2)
-            copy(out=dst[:, 2 * P * bp : 2 * P * (bp + 1), :], in_=xt[(g, bp)][:].rearrange("p u r -> p r u"))
-
-        def quant_x(g):
-            nc.vector.quantize_mx(out=xc[:, g, :].bitcast(FP8X4), scales=xs[:, g, :], in_=xg[g][:])
-
-        def mx(g, j):
-            if g == 0:
-                acc[j] = psum.tile([P, BATCH], F32, name="acc%d" % j, tag="bank%d" % j)
-            nc.tensor.matmul_mx(
-                out=acc[j][:],
-                lhsT=wc[:, g, j * P : (j + 1) * P].bitcast(FP8X4),
-                lhsT_scale=ws[:, g, j * P : (j + 1) * P],
-                rhs=xc[:, g, :].bitcast(FP8X4),
-                rhs_scale=xs[:, g, :],
-                start=(g == 0),
-                stop=(g == PASSES - 1),
+        def quantise_weights(g, lo, hi):
+            nc.vector.quantize_mx(
+                out=w_codes[:, g, lo:hi].bitcast(FP8X4),
+                scales=w_scales[:, g, lo:hi],
+                in_=w_words[g][:, lo:hi, :].rearrange("p w t -> p (w t)"),
             )
 
-        def th(j):
-            nc.scalar.activation(out=ot[j][:], in_=acc[j][:], func=ACT.Tanh, bias=b_half[:, j : j + 1], scale=0.5)
+        def flip_acts(o):
+            for pair in range(NB // 2):
+                for g in (2 * o, 2 * o + 1):
+                    bank = psum.tile([P, 2, 2 * P], F32, name="flipped%d_%d" % (g, pair), tag="bank%d" % (2 * g + pair))
+                    flipped[(g, pair)] = bank
+                    for u in range(2):
+                        for i in range(2):
+                            words = act_sb[o][:, 2 * pair + i, :].bitcast(F32)
+                            first = (K_PASS // 2) * (g % 2) + P * u
+                            nc.tensor.transpose(bank[:, u, i * P : (i + 1) * P], words[:, first : first + P], ident[:])
+            for pair in range(NB // 2):
+                for g in (2 * o, 2 * o + 1):
+                    dst = a_words[g][:].bitcast(F32).rearrange("p (r u) -> p r u", u=2)
+                    nc.scalar.copy(
+                        out=dst[:, 2 * P * pair : 2 * P * (pair + 1), :],
+                        in_=flipped[(g, pair)][:].rearrange("p u r -> p r u"),
+                    )
 
-        def to(j):
-            tp[j] = psum.tile([P, NB, P], F32, name="tp%d" % j, tag="bank%d" % j)
-            for b in range(NB):
-                nc.tensor.transpose(tp[j][:, b, :], ot[j][:, b * P : (b + 1) * P], ident[:])
+        def quantise_acts(g):
+            nc.vector.quantize_mx(out=a_codes[:, g, :].bitcast(FP8X4), scales=a_scales[:, g, :], in_=a_words[g][:])
 
-        def fm(j):
+        def spread_bias():
+            nc.vector.tensor_copy(out=bias_f32[:], in_=bias_rows[:])
+            nc.tensor.transpose(bias_ps[:], bias_f32[:], ident[:])
+            nc.vector.tensor_scalar_mul(out=bias_half[:], in0=bias_ps[:, 0:NJ], scalar1=0.5)
+
+        def log_n(b):
+            nc.scalar.activation(out=ratio[:, b, :], in_=n_sb[:, b, :], func=ACT.Ln, bias=eps2[:, 0:1], scale=2.0)
+
+        def reciprocal(b):
+            nc.scalar.activation(out=ratio[:, b, :], in_=ratio[:, b, :], func=ACT.Exp, scale=-1.0)
+
+        def times_c(b):
+            nc.vector.tensor_tensor(out=ratio[:, b, :], in0=c_sb[:, b, :], in1=ratio[:, b, :], op=ALU.mult)
+
+        def matmul_pass(g):
+            for j in range(NJ):
+                if g == 0:
+                    acc[j] = psum.tile([P, BATCH], F32, name="acc%d" % j, tag="bank%d" % j)
+                nc.tensor.matmul_mx(
+                    out=acc[j][:],
+                    lhsT=w_codes[:, g, j * P : (j + 1) * P].bitcast(FP8X4),
+                    lhsT_scale=w_scales[:, g, j * P : (j + 1) * P],
+                    rhs=a_codes[:, g, :].bitcast(FP8X4),
+                    rhs_scale=a_scales[:, g, :],
+                    start=(g == 0),
+                    stop=(g == PASSES - 1),
+                )
+
+        def finish(j):
             cols = slice(j * P, (j + 1) * P)
+            nc.scalar.activation(out=gate_t[j][:], in_=acc[j][:], func=ACT.Tanh, bias=bias_half[:, j : j + 1], scale=0.5)
+            gate[j] = psum.tile([P, NB, P], F32, name="gate%d" % j, tag="bank%d" % j)
+            for b in range(NB):
+                nc.tensor.transpose(gate[j][:, b, :], gate_t[j][:, b * P : (b + 1) * P], ident[:])
             nc.vector.scalar_tensor_tensor(
-                out=ho[:, :, cols], in0=tp[j][:], scalar=1.0, in1=rq[:, :, cols], op0=ALU.add, op1=ALU.mult
+                out=h_sb[:, :, cols], in0=gate[j][:], scalar=1.0, in1=ratio[:, :, cols], op0=ALU.add, op1=ALU.mult
             )
 
         def store(j0, j1):
             cols = slice(j0 * P, j1 * P)
-            nc.sync.dma_start(out=out_v[:, :, cols], in_=ho[:, :, cols])
+            nc.sync.dma_start(out=by_partition(out)[:, :, cols], in_=h_sb[:, :, cols])
 
+        half = FEAT // 2
         with tc.manual_schedule():
-            load_w(0, 0, 512)
+            load_weights(0, 0, half)
             load_rows(n_sb, n, 0, 1)
-            load_bias()
-            load_w(0, 512, 1024)
-            load_rows(n_sb, n, 1, 2)
-            load_rows(n_sb, n, 2, 3)
-            load_rows(n_sb, n, 3, 4)
-            load_w(1, 0, FEAT)
-            load_rows(a_sb[0], x, 0, 2)
-            load_rows(a_sb[0], x, 2, 4)
-            load_w(2, 0, FEAT)
-            load_rows(a_sb[1], h_prev, 0, 2)
-            load_rows(a_sb[1], h_prev, 2, 4)
-            load_w(3, 0, 512)
-            load_w(3, 512, 1024)
-            load_rows(c_sb, c, 0, 1)
-            load_rows(c_sb, c, 1, 2)
-            load_rows(c_sb, c, 2, 3)
-            load_rows(c_sb, c, 3, 4)
-            regroup(nc.vector.tensor_copy, 0, 0, 512)
-            ln(0)
-            bias_cast()
-            quant_w(0, 0, 512)
-            bias_flip()
-            regroup(nc.vector.tensor_copy, 0, 512, 1024)
-            ln(1)
-            bias_halve()
-            quant_w(0, 512, 1024)
-            ln(2)
-            ln(3)
-            regroup(nc.vector.tensor_copy, 1, 0, 928)
-            regroup(nc.scalar.copy, 1, 928, 1024)
-            flip(0, 0)
-            flip(1, 0)
-            flip(0, 1)
-            quant_w(1, 0, 1024)
-            flip_out(nc.scalar.copy, 0, 0)
-            flip(1, 1)
-            flip_out(nc.scalar.copy, 0, 1)
-            flip_out(nc.scalar.copy, 1, 0)
-            quant_x(0)
-            flip_out(nc.scalar.copy, 1, 1)
-            regroup(nc.vector.tensor_copy, 2, 0, 768)
-            mx(0, 0)
-            regroup(nc.scalar.copy, 2, 768, 1024)
-            mx(0, 1)
-            mx(0, 2)
-            flip(2, 0)
-            ex(0)
-            quant_x(1)
-            flip(3, 0)
-            mx(0, 3)
-            quant_w(2, 0, 1024)
-            flip(2, 1)
-            flip_out(nc.scalar.copy, 2, 0)
-            flip(3, 1)
-            mx(1, 0)
-            flip_out(nc.scalar.copy, 2, 1)
-            regroup(nc.vector.tensor_copy, 3, 0, 336)
-            mx(1, 1)
-            flip_out(nc.scalar.copy, 3, 0)
-            mx(1, 2)
-            mx(0, 4)
-            quant_x(2)
-            mx(1, 3)
-            flip_out(nc.scalar.copy, 3, 1)
-            mx(0, 5)
-            regroup(nc.vector.tensor_copy, 3, 512, 848)
-            mx(1, 4)
-            regroup(nc.scalar.copy, 3, 336, 512)
-            mx(0, 6)
-            mx(1, 5)
-            quant_x(3)
-            mx(0, 7)
-            regroup(nc.scalar.copy, 3, 848, 1024)
-            mx(1, 6)
-            quant_w(3, 0, 512)
-            mx(2, 0)
-            mx(1, 7)
-            ex(1)
-            cr(0)
-            mx(2, 1)
-            mx(2, 2)
-            mx(2, 3)
-            mx(2, 4)
-            ex(2)
-            quant_w(3, 512, 1024)
-            mx(2, 5)
-            mx(2, 6)
-            cr(1)
-            mx(2, 7)
-            mx(3, 0)
-            ex(3)
-            mx(3, 1)
-            mx(3, 2)
-            cr(2)
-            mx(3, 3)
-            mx(3, 4)
-            th(0)
-            mx(3, 5)
-            mx(3, 6)
-            th(1)
-            cr(3)
-            mx(3, 7)
-            to(0)
-            th(2)
-            to(1)
-            th(3)
-            to(2)
-            fm(0)
-            th(4)
-            to(3)
-            fm(1)
-            th(5)
-            to(4)
-            fm(2)
-            store(0, 2)
-            th(6)
-            to(5)
-            fm(3)
-            th(7)
-            to(6)
-            fm(4)
-            store(2, 4)
-            to(7)
-            fm(5)
-            fm(6)
-            store(4, 6)
-            fm(7)
-            store(6, 7)
-            store(7, 8)
+            nc.sync.dma_start(out=bias_rows[0:NJ, :], in_=b_o.rearrange("(j p) -> j p", p=P))
+            load_weights(0, half, FEAT)
+            for b in range(1, NB):
+                load_rows(n_sb, n, b, b + 1)
+            load_weights(1, 0, FEAT)
+            load_rows(act_sb[0], x, 0, 2)
+            load_rows(act_sb[0], x, 2, 4)
+            load_weights(2, 0, FEAT)
+            load_rows(act_sb[1], h_prev, 0, 2)
+            load_rows(act_sb[1], h_prev, 2, 4)
+            load_weights(3, 0, half)
+            load_weights(3, half, FEAT)
+            for b in range(NB):
+                load_rows(c_sb, c, b, b + 1)
+
+            interleave(0, 0, half)
+            quantise_weights(0, 0, half)
+            interleave(0, half, FEAT)
+            quantise_weights(0, half, FEAT)
+            spread_bias()
+            for b in range(NB):
+                log_n(b)
+            interleave(1, 0, FEAT)
+            reciprocal(0)
+            quantise_weights(1, 0, FEAT)
+            flip_acts(0)
+            interleave(2, 0, FEAT)
+            quantise_acts(0)
+            quantise_acts(1)
+            quantise_weights(2, 0, FEAT)
+            flip_acts(1)
+            interleave(3, 0, half)
+            interleave(3, half, FEAT)
+            quantise_acts(2)
+            quantise_acts(3)
+            quantise_weights(3, 0, half)
+            quantise_weights(3, half, FEAT)
+            for b in range(1, NB):
+                reciprocal(b)
+            for b in range(NB):
+                times_c(b)
+            for g in range(PASSES):
+                matmul_pass(g)
+            for j in range(NJ):
+                finish(j)
+                if j in (1, 3, 5):
+                    store(j - 1, j + 1)
+                if j >= NJ - 2:
+                    store(j, j + 1)

@@ -66,28 +66,28 @@ def tile_slstmcell_pb_kernel(tc, x, h_prev, c, n, W_o, b_o, U_o, out):
         def load_rows(dst, src, lo, hi):
             nc.sync.dma_start(out=dst[:, lo:hi, :], in_=by_partition(src)[:, lo:hi, :])
 
-        def load_weights(g, lo, hi):
+        def load_weights(g):
             rows = weights[g // 2][K_PASS * (g % 2) : K_PASS * (g % 2 + 1), :]
             for u in range(2):
                 nc.sync.dma_start(
-                    out=w_rows[g][:, 2 * u : 2 * u + 2, lo:hi],
-                    in_=rows[2 * P * u : 2 * P * (u + 1), lo:hi].rearrange("(p e) w -> p e w", e=2),
+                    out=w_rows[g][:, 2 * u : 2 * u + 2, :],
+                    in_=rows[2 * P * u : 2 * P * (u + 1), :].rearrange("(p e) w -> p e w", e=2),
                 )
 
-        def interleave(g, lo, hi):
-            cut = hi - SCALAR_COLS[g] * (hi - lo) // FEAT
-            for copy, a, b in ((nc.vector.tensor_copy, lo, cut), (nc.scalar.copy, cut, hi)):
+        def interleave(g):
+            cut = FEAT - SCALAR_COLS[g]
+            for copy, a, b in ((nc.vector.tensor_copy, 0, cut), (nc.scalar.copy, cut, FEAT)):
                 if b > a:
                     copy(
                         out=w_words[g][:, a:b, :].rearrange("p (w i) t -> p w t i", i=4),
                         in_=w_rows[g][:, :, a:b].rearrange("p t (w i) -> p w t i", i=4),
                     )
 
-        def quantise_weights(g, lo, hi):
+        def quantise_weights(g):
             nc.vector.quantize_mx(
-                out=w_codes[:, g, lo:hi].bitcast(FP8X4),
-                scales=w_scales[:, g, lo:hi],
-                in_=w_words[g][:, lo:hi, :].rearrange("p w t -> p (w t)"),
+                out=w_codes[:, g, :].bitcast(FP8X4),
+                scales=w_scales[:, g, :],
+                in_=w_words[g][:].rearrange("p w t -> p (w t)"),
             )
 
         def flip_acts(o):
@@ -153,47 +153,36 @@ def tile_slstmcell_pb_kernel(tc, x, h_prev, c, n, W_o, b_o, U_o, out):
             cols = slice(j0 * P, j1 * P)
             nc.sync.dma_start(out=by_partition(out)[:, :, cols], in_=h_sb[:, :, cols])
 
-        half = FEAT // 2
         with tc.manual_schedule():
-            load_weights(0, 0, half)
             load_rows(n_sb, n, 0, 1)
+            load_weights(0)
             nc.sync.dma_start(out=bias_rows[0:NJ, :], in_=b_o.rearrange("(j p) -> j p", p=P))
-            load_weights(0, half, FEAT)
             for b in range(1, NB):
                 load_rows(n_sb, n, b, b + 1)
-            load_weights(1, 0, FEAT)
+            load_weights(1)
             load_rows(act_sb[0], x, 0, 2)
             load_rows(act_sb[0], x, 2, 4)
-            load_weights(2, 0, FEAT)
+            load_weights(2)
             load_rows(act_sb[1], h_prev, 0, 2)
             load_rows(act_sb[1], h_prev, 2, 4)
-            load_weights(3, 0, half)
-            load_weights(3, half, FEAT)
-            for b in range(NB):
-                load_rows(c_sb, c, b, b + 1)
+            load_weights(3)
+            load_rows(c_sb, c, 0, 2)
+            load_rows(c_sb, c, 2, 4)
 
-            interleave(0, 0, half)
-            quantise_weights(0, 0, half)
-            interleave(0, half, FEAT)
-            quantise_weights(0, half, FEAT)
-            spread_bias()
             for b in range(NB):
                 log_n(b)
-            interleave(1, 0, FEAT)
+            interleave(0)
+            quantise_weights(0)
+            spread_bias()
+            interleave(1)
             reciprocal(0)
-            quantise_weights(1, 0, FEAT)
-            flip_acts(0)
-            interleave(2, 0, FEAT)
-            quantise_acts(0)
-            quantise_acts(1)
-            quantise_weights(2, 0, FEAT)
-            flip_acts(1)
-            interleave(3, 0, half)
-            interleave(3, half, FEAT)
-            quantise_acts(2)
-            quantise_acts(3)
-            quantise_weights(3, 0, half)
-            quantise_weights(3, half, FEAT)
+            quantise_weights(1)
+            for o in range(2):
+                flip_acts(o)
+                interleave(2 + o)
+                quantise_acts(2 * o)
+                quantise_acts(2 * o + 1)
+                quantise_weights(2 + o)
             for b in range(1, NB):
                 reciprocal(b)
             for b in range(NB):
@@ -202,7 +191,5 @@ def tile_slstmcell_pb_kernel(tc, x, h_prev, c, n, W_o, b_o, U_o, out):
                 matmul_pass(g)
             for j in range(NJ):
                 finish(j)
-                if j in (1, 3, 5):
+                if j % 2 == 1:
                     store(j - 1, j + 1)
-                if j >= NJ - 2:
-                    store(j, j + 1)

from contextlib import ExitStack

import concourse.masks as masks
import concourse.mybir as mybir

F32 = mybir.dt.float32
BF16 = mybir.dt.bfloat16
U32 = mybir.dt.uint32
U8 = mybir.dt.uint8
FP8X4 = mybir.dt.float8_e4m3fn_x4
ACT = mybir.ActivationFunctionType
ALU = mybir.AluOpType

P = 128
BATCH = 512
FEAT = 1024
NB = BATCH // P
NJ = FEAT // P
K_PASS = 4 * P
PASSES = 2 * FEAT // K_PASS
EPS = 1e-6

SCALAR_COLS = (0, 0, 256, 512)

FLOPS = 2 * BATCH * FEAT * FEAT * 2


def tile_slstmcell_pb_kernel(tc, x, h_prev, c, n, W_o, b_o, U_o, out):
    nc = tc.nc
    with ExitStack() as ctx:
        keep = ctx.enter_context(tc.tile_pool(name="keep", bufs=1))
        psum = ctx.enter_context(tc.psum_pool(name="psum", bufs=1))

        ident = keep.tile([P, P], F32, name="ident")
        masks.make_identity(nc, ident[:])
        eps2 = keep.tile([P, 1], F32, name="eps2")
        nc.vector.memset(eps2[:], 2.0 * EPS)
        bias_rows = keep.tile([P, P], BF16, name="bias_rows")
        nc.vector.memset(bias_rows[:], 0.0)

        acts = [x, h_prev]
        weights = [W_o, U_o]
        act_sb = [keep.tile([P, NB, FEAT], BF16, name="act_sb%d" % o) for o in range(2)]
        n_sb = keep.tile([P, NB, FEAT], BF16, name="n_sb")
        c_sb = keep.tile([P, NB, FEAT], BF16, name="c_sb")
        w_rows = [keep.tile([P, 4, FEAT], BF16, name="w_rows%d" % g) for g in range(PASSES)]
        w_words = [keep.tile([P, FEAT, 4], BF16, name="w_words%d" % g, align_bytes=64) for g in range(PASSES)]
        w_codes = keep.tile([P, PASSES, FEAT], U32, name="w_codes", align_bytes=64)
        w_scales = keep.tile([P, PASSES, FEAT], U8, name="w_scales", align_bytes=64)
        a_words = [keep.tile([P, BATCH * 4], BF16, name="a_words%d" % g, align_bytes=64) for g in range(PASSES)]
        a_codes = keep.tile([P, PASSES, BATCH], U32, name="a_codes", align_bytes=64)
        a_scales = keep.tile([P, PASSES, BATCH], U8, name="a_scales", align_bytes=64)
        ratio = keep.tile([P, NB, FEAT], F32, name="ratio")
        gate_t = [keep.tile([P, BATCH], F32, name="gate_t%d" % j) for j in range(NJ)]
        h_sb = keep.tile([P, NB, FEAT], F32, name="h_sb")
        bias_f32 = keep.tile([P, P], F32, name="bias_f32")
        bias_half = keep.tile([P, NJ], F32, name="bias_half")
        bias_ps = psum.tile([P, P], F32, name="bias_ps", tag="bank7")
        flipped = {}
        acc = {}
        gate = {}

        def by_partition(rows):
            return rows.rearrange("(p b) d -> p b d", b=NB)

        def load_rows(dst, src, lo, hi):
            nc.sync.dma_start(out=dst[:, lo:hi, :], in_=by_partition(src)[:, lo:hi, :])

        def load_weights(g):
            rows = weights[g // 2][K_PASS * (g % 2) : K_PASS * (g % 2 + 1), :]
            for u in range(2):
                nc.sync.dma_start(
                    out=w_rows[g][:, 2 * u : 2 * u + 2, :],
                    in_=rows[2 * P * u : 2 * P * (u + 1), :].rearrange("(p e) w -> p e w", e=2),
                )

        def interleave(g):
            cut = FEAT - SCALAR_COLS[g]
            for copy, a, b in ((nc.vector.tensor_copy, 0, cut), (nc.scalar.copy, cut, FEAT)):
                if b > a:
                    copy(
                        out=w_words[g][:, a:b, :].rearrange("p (w i) t -> p w t i", i=4),
                        in_=w_rows[g][:, :, a:b].rearrange("p t (w i) -> p w t i", i=4),
                    )

        def quantise_weights(g):
            nc.vector.quantize_mx(
                out=w_codes[:, g, :].bitcast(FP8X4),
                scales=w_scales[:, g, :],
                in_=w_words[g][:].rearrange("p w t -> p (w t)"),
            )

        def flip_acts(o):
            for pair in range(NB // 2):
                for g in (2 * o, 2 * o + 1):
                    bank = psum.tile([P, 2, 2 * P], F32, name="flipped%d_%d" % (g, pair), tag="bank%d" % (2 * g + pair))
                    flipped[(g, pair)] = bank
                    for u in range(2):
                        for i in range(2):
                            words = act_sb[o][:, 2 * pair + i, :].bitcast(F32)
                            first = (K_PASS // 2) * (g % 2) + P * u
                            nc.tensor.transpose(bank[:, u, i * P : (i + 1) * P], words[:, first : first + P], ident[:])
            for pair in range(NB // 2):
                for g in (2 * o, 2 * o + 1):
                    dst = a_words[g][:].bitcast(F32).rearrange("p (r u) -> p r u", u=2)
                    nc.scalar.copy(
                        out=dst[:, 2 * P * pair : 2 * P * (pair + 1), :],
                        in_=flipped[(g, pair)][:].rearrange("p u r -> p r u"),
                    )

        def quantise_acts(g):
            nc.vector.quantize_mx(out=a_codes[:, g, :].bitcast(FP8X4), scales=a_scales[:, g, :], in_=a_words[g][:])

        def spread_bias():
            nc.vector.tensor_copy(out=bias_f32[:], in_=bias_rows[:])
            nc.tensor.transpose(bias_ps[:], bias_f32[:], ident[:])
            nc.vector.tensor_scalar_mul(out=bias_half[:], in0=bias_ps[:, 0:NJ], scalar1=0.5)

        def log_n(b):
            nc.scalar.activation(out=ratio[:, b, :], in_=n_sb[:, b, :], func=ACT.Ln, bias=eps2[:, 0:1], scale=2.0)

        def reciprocal(b):
            nc.scalar.activation(out=ratio[:, b, :], in_=ratio[:, b, :], func=ACT.Exp, scale=-1.0)

        def times_c(b):
            nc.vector.tensor_tensor(out=ratio[:, b, :], in0=c_sb[:, b, :], in1=ratio[:, b, :], op=ALU.mult)

        def matmul_pass(g):
            for j in range(NJ):
                if g == 0:
                    acc[j] = psum.tile([P, BATCH], F32, name="acc%d" % j, tag="bank%d" % j)
                nc.tensor.matmul_mx(
                    out=acc[j][:],
                    lhsT=w_codes[:, g, j * P : (j + 1) * P].bitcast(FP8X4),
                    lhsT_scale=w_scales[:, g, j * P : (j + 1) * P],
                    rhs=a_codes[:, g, :].bitcast(FP8X4),
                    rhs_scale=a_scales[:, g, :],
                    start=(g == 0),
                    stop=(g == PASSES - 1),
                )

        def finish(j):
            cols = slice(j * P, (j + 1) * P)
            nc.scalar.activation(out=gate_t[j][:], in_=acc[j][:], func=ACT.Tanh, bias=bias_half[:, j : j + 1], scale=0.5)
            gate[j] = psum.tile([P, NB, P], F32, name="gate%d" % j, tag="bank%d" % j)
            for b in range(NB):
                nc.tensor.transpose(gate[j][:, b, :], gate_t[j][:, b * P : (b + 1) * P], ident[:])
            nc.vector.scalar_tensor_tensor(
                out=h_sb[:, :, cols], in0=gate[j][:], scalar=1.0, in1=ratio[:, :, cols], op0=ALU.add, op1=ALU.mult
            )

        def store(j0, j1):
            cols = slice(j0 * P, j1 * P)
            nc.sync.dma_start(out=by_partition(out)[:, :, cols], in_=h_sb[:, :, cols])

        with tc.manual_schedule():
            load_rows(n_sb, n, 0, 1)
            load_weights(0)
            nc.sync.dma_start(out=bias_rows[0:NJ, :], in_=b_o.rearrange("(j p) -> j p", p=P))
            for b in range(1, NB):
                load_rows(n_sb, n, b, b + 1)
            load_weights(1)
            load_rows(act_sb[0], x, 0, 2)
            load_rows(act_sb[0], x, 2, 4)
            load_weights(2)
            load_rows(act_sb[1], h_prev, 0, 2)
            load_rows(act_sb[1], h_prev, 2, 4)
            load_weights(3)
            load_rows(c_sb, c, 0, 2)
            load_rows(c_sb, c, 2, 4)

            for b in range(NB):
                log_n(b)
            interleave(0)
            quantise_weights(0)
            spread_bias()
            interleave(1)
            reciprocal(0)
            quantise_weights(1)
            for o in range(2):
                flip_acts(o)
                interleave(2 + o)
                quantise_acts(2 * o)
                quantise_acts(2 * o + 1)
                quantise_weights(2 + o)
            for b in range(1, NB):
                reciprocal(b)
            for b in range(NB):
                times_c(b)
            for g in range(PASSES):
                matmul_pass(g)
            for j in range(NJ):
                finish(j)
                if j % 2 == 1:
                    store(j - 1, j + 1)
